import numpy as np
import ml_dtypes


def mxq(x, axis, fmt="e4m3"):
    dtype, down = {"e4m3": (ml_dtypes.float8_e4m3fn, 7), "e5m2": (ml_dtypes.float8_e5m2, 14)}[fmt]
    v = np.moveaxis(np.asarray(x, np.float32).astype(ml_dtypes.bfloat16).astype(np.float64), axis, -1)
    blocks = v.reshape(v.shape[:-1] + (-1, 32))
    amax = np.abs(blocks).max(-1, keepdims=True)
    byte = np.maximum(np.where(amax > 0, np.frexp(amax)[1] - 1 + 127, 0) - down, 1)
    scale = np.exp2(byte - 127.0)
    codes = (blocks / scale).astype(np.float32).astype(dtype).astype(np.float64)
    return np.moveaxis((codes * scale).reshape(v.shape), -1, axis)


WIDE = False


def mx_kscale(k):
    if not WIDE:
        return np.ones(k)
    levels = np.array([10, -10, 5, -5, 0])
    if k % 512:
        return np.exp2(np.random.permutation(np.resize(levels, k // 32))).repeat(32)
    a = np.empty((k // 512, 16))
    for p in range(k // 512):
        a[p, :8] = np.random.permutation(np.resize(levels, 8))
        for g in range(8):
            far = levels[np.abs(levels - a[p, g]) >= 10]
            a[p, g + 8] = far[np.random.randint(len(far))]
    return np.exp2(a.ravel()).repeat(32)


BF16 = ml_dtypes.bfloat16


def bf(x):
    return np.asarray(x, np.float32).astype(BF16)


def f64(x):
    return np.asarray(x).astype(np.float64)


E2M1 = np.array([0.0, 0.5, 1.0, 1.5, 2.0, 3.0, 4.0, 6.0, -0.0, -0.5, -1.0, -1.5, -2.0, -3.0, -4.0, -6.0])


def pack_weight(w, fmt):
    k, n = w.shape
    w = f64(bf(w)).reshape(k // 32, 32, n)
    amax = np.abs(w).max(1)
    if fmt == "e4m3":
        byte = np.frexp(amax)[1] - 1 + 127 - 7
    else:
        mant, ex = np.frexp(amax / 6.0)
        byte = np.where(mant > 0.5, ex, ex - 1) + 127
    byte = np.clip(np.where(amax > 0, byte, 1), 1, 254)
    scaled = (w * np.exp2(127.0 - byte)[:, None, :]).reshape(k, n).astype(np.float32)
    by_word = np.ascontiguousarray(scaled.reshape(k // 512, 128, 4, n).transpose(0, 1, 3, 2))
    if fmt == "e4m3":
        words = by_word.astype(ml_dtypes.float8_e4m3fn).view(np.uint8)
    else:
        c = by_word.astype(ml_dtypes.float4_e2m1fn).view(np.uint8) & 0xF
        words = c[..., 0::2] | (c[..., 1::2] << 4)
    return np.ascontiguousarray(words), np.ascontiguousarray(byte.astype(np.uint8).reshape(k // 512, 16, n))


def unpack_weight(words, scales, fmt):
    g, p, n, _ = words.shape
    if fmt == "e4m3":
        vals = np.ascontiguousarray(words).view(ml_dtypes.float8_e4m3fn).astype(np.float64)
    else:
        nib = np.empty((g, p, n, 4), np.uint8)
        nib[..., 0::2] = words & 0xF
        nib[..., 1::2] = words >> 4
        vals = E2M1[nib]
    vals = vals * np.repeat(np.exp2(scales.astype(np.float64) - 127.0), 8, axis=1)[..., None]
    return vals.transpose(0, 1, 3, 2).reshape(g * 512, n)
def pack4(w):
    words, scales = pack_weight(w, "e2m1")
    return words.reshape(words.shape[0], 128, -1), scales


def unpack4(words, scales):
    return unpack_weight(words.reshape(words.shape[0], 128, -1, 2), scales, "e2m1")


B, RES, C, NH, RD, RW = 4, 32, 512, 8, 16, 128
N, L = B * RES, RES


def draw0():
    s, t = mx_kscale(C), mx_kscale(C)
    y_h = bf(np.random.standard_normal((N, L, C)) * 0.5 * s)
    y_w = bf(np.random.standard_normal((N, L, C)) * 0.5 * s)
    x = bf(np.random.standard_normal((B, RES, RES, C)) * s)
    a_logits = bf(np.random.standard_normal((B, 3 * C)))
    Wo_h_words, Wo_h_scales = pack4((np.random.standard_normal((C, C)) * 2.0 / np.sqrt(C) * t[:, None] / s).T)
    bo_h = bf(np.random.standard_normal(C) * 0.3 * t)
    Wo_w_words, Wo_w_scales = pack4((np.random.standard_normal((C, C)) * 2.0 / np.sqrt(C) * t[:, None] / s).T)
    bo_w = bf(np.random.standard_normal(C) * 0.3 * t)
    Wmlpc_words, Wmlpc_scales = pack4((np.random.standard_normal((C, C)) / np.sqrt(C) * t[:, None] / s).T)
    Wp_words, Wp_scales = pack4((np.random.standard_normal((C, C)) * 1.5 / np.sqrt(C) / t).T)
    bp = bf(np.random.standard_normal(C) * 0.3)
    return {"y_h": y_h,
            "y_w": y_w,
            "x": x,
            "a_logits": a_logits,
            "Wo_h_words": Wo_h_words,
            "Wo_h_scales": Wo_h_scales,
            "bo_h": bo_h,
            "Wo_w_words": Wo_w_words,
            "Wo_w_scales": Wo_w_scales,
            "bo_w": bo_w,
            "Wmlpc_words": Wmlpc_words,
            "Wmlpc_scales": Wmlpc_scales,
            "Wp_words": Wp_words,
            "Wp_scales": Wp_scales,
            "bp": bp}


def core(y_h, y_w, x, a_logits, Wo_h_words, Wo_h_scales, bo_h, Wo_w_words, Wo_w_scales, bo_w, Wmlpc_words, Wmlpc_scales, Wp_words, Wp_scales, bp):
    h = (mxq(f64(y_h), 2, "e4m3") @ unpack4(Wo_h_words, Wo_h_scales)) + f64(bo_h)
    h = h.reshape(B, RES, RES, C).transpose(0, 2, 1, 3)
    w = (mxq(f64(y_w), 2, "e4m3") @ unpack4(Wo_w_words, Wo_w_scales)) + f64(bo_w)
    w = w.reshape(B, RES, RES, C)
    c = mxq(f64(x), 3, "e4m3") @ unpack4(Wmlpc_words, Wmlpc_scales)
    a = f64(a_logits).reshape(B, C, 3).transpose(2, 0, 1)
    a = np.exp(a - a.max(0, keepdims=True))
    a = (a / a.sum(0, keepdims=True))[:, :, None, None, :]
    out = h * a[0] + w * a[1] + c * a[2]
    return (mxq(out, 3, "e4m3") @ unpack4(Wp_words, Wp_scales)) + f64(bp)


def e4m3fn_bytes(y):
    return np.clip(np.asarray(y, np.float64), -448.0, 448.0).astype(np.float32).astype(ml_dtypes.float8_e4m3fn).view(np.uint8)


def e4m3fn_values(b):
    return np.asarray(b, np.uint8).view(ml_dtypes.float8_e4m3fn).astype(np.float64)


def setup_inputs():
    d = draw0()
    x0 = np.asarray(d['y_w']).astype(np.float64)
    s = (np.max(np.abs(x0), axis=(0, 1), keepdims=True) / 448.0).astype(np.float32)
    out = {}
    for k, v in d.items():
        if k == 'y_w':
            out['y_w_bytes'] = e4m3fn_bytes(x0 / s.astype(np.float64))
            out['y_w_scale'] = s
        else:
            out[k] = v
    return out


def reference(y_h, y_w_bytes, y_w_scale, x, a_logits, Wo_h_words, Wo_h_scales, bo_h, Wo_w_words, Wo_w_scales, bo_w, Wmlpc_words, Wmlpc_scales, Wp_words, Wp_scales, bp):
    return core(y_h, e4m3fn_values(y_w_bytes) * y_w_scale.astype(np.float64), x, a_logits, Wo_h_words, Wo_h_scales, bo_h, Wo_w_words, Wo_w_scales, bo_w, Wmlpc_words, Wmlpc_scales, Wp_words, Wp_scales, bp)

@@ -1,0 +1,431 @@
+from contextlib import ExitStack
+
+import concourse.mybir as mybir
+from concourse.masks import make_identity
+
+F32 = mybir.dt.float32
+BF16 = mybir.dt.bfloat16
+U8 = mybir.dt.uint8
+U32 = mybir.dt.uint32
+I32 = mybir.dt.int32
+FP8 = mybir.dt.float8_e4m3fn
+FP8X4 = mybir.dt.float8_e4m3fn_x4
+FP4X4 = mybir.dt.float4_e2m1fn_x4
+ADD = mybir.AluOpType.add
+SUB = mybir.AluOpType.subtract
+MULT = mybir.AluOpType.mult
+MAX = mybir.AluOpType.max
+ACT = mybir.ActivationFunctionType
+X_AXIS = mybir.AxisListType.X
+
+B, RES, C = 4, 32, 512
+P = 128
+SLOTS = 8
+NT = 4
+PAIR_BUFS = 3
+CAST_MORE = 1
+CODE_BUFS = 3
+FLOPS = 2 * 4 * B * RES * RES * C * C
+
+
+def tile_dynamixerblock_pb_w4_kernel(
+    tc,
+    y_h,
+    y_w_bytes,
+    y_w_scale,
+    x,
+    a_logits,
+    wh_words,
+    wh_scales,
+    bo_h,
+    ww_words,
+    ww_scales,
+    bo_w,
+    wc_words,
+    wc_scales,
+    wp_words,
+    wp_scales,
+    bp,
+    out,
+):
+    nc = tc.nc
+    halves = 4 * B
+    x_rows = x.rearrange("b i j c -> b (i j) c")
+    out_rows = out.rearrange("b i j c -> b (i j) c")
+    yw_rows = y_w_bytes.rearrange("(b i) j c -> b (i j) c", b=B)
+
+    with ExitStack() as ctx:
+        const = ctx.enter_context(tc.tile_pool(name="const", bufs=1))
+        stream = ctx.enter_context(tc.tile_pool(name="stream", bufs=2))
+        psum_t = ctx.enter_context(tc.psum_pool(name="psum_t", bufs=3))
+        psum_m = ctx.enter_context(tc.psum_pool(name="psum_m", bufs=5))
+        ctx.enter_context(tc.manual_schedule())
+
+        ident = const.tile([P, P], F32, name="ident")
+        perm = const.tile([P, P], F32, name="perm")
+        warm = const.tile([P, 1], F32, name="warm")
+        w_raw = const.tile([P, 4, 2 * C], U8, name="w_raw", align_bytes=64)
+        s_raw = const.tile([P, 4, C], U8, name="s_raw", align_bytes=64)
+        w_perm = const.tile([P, 3, 2 * C], U8, name="w_perm", align_bytes=64)
+        s_perm = const.tile([P, 3, C], U8, name="s_perm", align_bytes=64)
+        logits = const.tile([P, B, NT, 3], BF16, name="logits")
+        top = const.tile([P, B, NT], F32, name="top")
+        total = const.tile([P, B, NT], F32, name="total")
+        coef = const.tile([P, B, NT, 3], F32, name="coef")
+        beta = const.tile([P, B, NT], F32, name="beta")
+        beta_w = const.tile([P, B, NT], F32, name="beta_w")
+        bias_h = const.tile([P, NT], BF16, name="bias_h")
+        bias_w = const.tile([P, NT], BF16, name="bias_w")
+        bias_p = const.tile([P, C], BF16, name="bias_p")
+        yw_scale = const.tile([P, NT], F32, name="yw_scale")
+        x_sb = []
+        yh_sb = []
+        yb_sb = []
+        for b in range(B):
+            x_b = const.tile([P, SLOTS, C], BF16, name="x_sb%d" % b)
+            yh_b = const.tile([P, SLOTS, C], BF16, name="yh_sb%d" % b)
+            yb_b = const.tile([P, SLOTS, C], U8, name="yb_sb%d" % b)
+            x_sb.append(x_b)
+            yh_sb.append(yh_b)
+            yb_sb.append(yb_b)
+
+        def load_x(b, s0, s1):
+            nc.sync.dma_start(out=x_sb[b][:, s0:s1, :], in_=x_rows[b].rearrange("(p s) c -> p s c", s=SLOTS)[:, s0:s1, :])
+
+        def load_yb(b, s0, s1):
+            nc.sync.dma_start(out=yb_sb[b][:, s0:s1, :], in_=yw_rows[b].rearrange("(p s) c -> p s c", s=SLOTS)[:, s0:s1, :])
+
+        def load_yh(b, s0, s1, queue):
+            for jq in range(4):
+                r0 = b * RES + SLOTS * jq
+                queue.dma_start(
+                    out=yh_sb[b][32 * jq : 32 * jq + 32, s0:s1, :],
+                    in_=y_h[r0 + s0 : r0 + s1].rearrange("s i c -> i s c"),
+                )
+
+        def load_w(n, words, scales):
+            nc.sync.dma_start(out=w_raw[:, n, :], in_=words[0])
+            for q in range(4):
+                nc.sync.dma_start(
+                    out=s_raw[32 * q : 32 * q + 4, n, :].bitcast(I32),
+                    in_=scales[0, 4 * q : 4 * q + 4, :].bitcast(I32),
+                )
+
+        def permute_w(n):
+            nc.vector.tensor_copy(
+                out=w_perm[:, n, :].rearrange("p (t m e) -> p t m e", t=NT, e=2),
+                in_=w_raw[:, n, :].rearrange("p (m t e) -> p t m e", t=NT, e=2),
+            )
+            nc.vector.tensor_copy(
+                out=s_perm[:, n, :].rearrange("p (t m) -> p t m", t=NT),
+                in_=s_raw[:, n, :].rearrange("p (m t) -> p t m", t=NT),
+            )
+
+        cast_t = {}
+        bank_t = {}
+        pair_t = {}
+        codes_t = {}
+        mix_h = {}
+        mix_w = {}
+
+        def cast_yw(k):
+            b, s0 = k // 4, 2 * (k % 4)
+            yw = stream.tile([P, 2, C], BF16, name="yw_cast", bufs=4)
+            nc.scalar.activation(
+                out=yw[:].rearrange("p s c -> p (s c)"),
+                in_=yb_sb[b][:, s0 : s0 + 2, :].rearrange("p s c -> p (s c)").bitcast(FP8),
+                func=ACT.Copy,
+            )
+            cast_t[k] = yw
+
+        def transposes(k, which):
+            b, s0 = k // 4, 2 * (k % 4)
+            if which == "x":
+                src = x_sb[b][:, s0 : s0 + 2, :]
+            elif which == "h":
+                src = yh_sb[b][:, s0 : s0 + 2, :]
+            else:
+                src = cast_t[k][:]
+            bank = psum_t.tile([P, 2, 2, P], F32, name="bank")
+            for s in range(2):
+                words = src[:, s, :].bitcast(F32)
+                for u in range(2):
+                    nc.tensor.transpose(bank[:, u, s, :], words[:, u : 2 * P : 2], perm[:] if which == "h" else ident[:])
+            bank_t[k, which] = bank
+
+        def pair(name, g):
+            if (name, g) not in pair_t:
+                tile = stream.tile([P, 2, C, NT], BF16, name="pair_" + name, align_bytes=64, bufs=PAIR_BUFS)
+                pair_t[name, g] = tile
+            return pair_t[name, g]
+
+        def evacuate(k, which, on_vector=False):
+            bank = bank_t.pop((k, which))
+            g, half = k // 2, k % 2
+            cols = slice(2 * P * half, 2 * P * (half + 1))
+            if which == "w":
+                nc.vector.tensor_tensor(
+                    out=pair("E", g)[:, 0, cols, :].rearrange("p n (u e) -> p n u e", e=2),
+                    in0=bank[:].rearrange("p u s r -> p (u s r)").bitcast(BF16).rearrange("p (u n e) -> p n u e", u=2, e=2),
+                    in1=yw_scale[:].rearrange("p (u e) -> p u e", e=2).unsqueeze(1).to_broadcast([P, 2 * P, 2, 2]),
+                    op=MULT,
+                )
+            else:
+                dst = pair("L", g)[:, 0, cols, :] if which == "x" else pair("E", g)[:, 1, cols, :]
+                dst = dst.rearrange("p n t -> p (n t)").bitcast(F32).rearrange("p (n u) -> p n u", u=2)
+                words = bank[:].rearrange("p u s r -> p (s r) u")
+                if on_vector:
+                    nc.vector.tensor_copy(out=dst, in_=words)
+                else:
+                    nc.scalar.copy(out=dst, in_=words)
+
+        def quantize(name, g, i0, i1, c0=0, c1=C):
+            if (name, g) not in codes_t:
+                codes = stream.tile([P, 2, C], U32, name="codes_" + name, align_bytes=64, bufs=CODE_BUFS)
+                scales = stream.tile([P, 2, C], U8, name="scales_" + name, align_bytes=64, bufs=CODE_BUFS)
+                codes_t[name, g] = (codes, scales)
+            codes, scales = codes_t[name, g]
+            nc.vector.quantize_mx(
+                out=codes[:, i0:i1, c0:c1].rearrange("p i c -> p (i c)").bitcast(FP8X4),
+                scales=scales[:, i0:i1, c0:c1].rearrange("p i c -> p (i c)"),
+                in_=pair(name, g)[:, i0:i1, c0:c1, :].rearrange("p i n t -> p (i n t)"),
+            )
+
+        OPERAND = {"x": ("L", 0, 2), "w": ("E", 0, 1), "h": ("E", 1, 0)}
+
+        def project(g, t, which, c0, c1):
+            name, i, n = OPERAND[which]
+            codes, scales = codes_t[name, g]
+            acc = psum_m.tile([P, C], F32, name="acc")
+            nc.tensor.matmul_mx(
+                out=acc[:, 0 : c1 - c0],
+                lhsT=w_perm[:, n, 2 * P * t : 2 * P * (t + 1)].bitcast(FP4X4),
+                lhsT_scale=s_perm[:, n, P * t : P * (t + 1)],
+                rhs=codes[:, i, c0:c1].bitcast(FP8X4),
+                rhs_scale=scales[:, i, c0:c1],
+                start=True,
+                stop=True,
+            )
+            return acc
+
+        part = {}
+
+        def mix(g, t, which, acc, c0, c1):
+            b = g // 2
+            if g not in mix_h:
+                mh = stream.tile([P, NT, C], F32, name="mh")
+                mw = stream.tile([P, NT, C], F32, name="mw")
+                mix_h[g] = mh
+                mix_w[g] = mw
+            if which == "x":
+                part_c = stream.tile([P, C], F32, name="part_c", bufs=4)
+                part[t] = part_c
+                nc.scalar.activation(out=part_c[:, 0 : c1 - c0], in_=acc[:, 0 : c1 - c0], func=ACT.Copy, scale=coef[:, b, t, 2:3])
+            elif which == "w":
+                nc.vector.scalar_tensor_tensor(
+                    out=mix_w[g][:, t, c0:c1],
+                    in0=acc[:, 0 : c1 - c0],
+                    scalar=coef[:, b, t, 1:2],
+                    in1=part[t][:, 0 : c1 - c0],
+                    op0=MULT,
+                    op1=ADD,
+                )
+            else:
+                nc.scalar.activation(
+                    out=mix_h[g][:, t, c0:c1],
+                    in_=acc[:, 0 : c1 - c0],
+                    func=ACT.Identity,
+                    bias=beta[:, b, t : t + 1],
+                    scale=coef[:, b, t, 0:1],
+                )
+
+        def blend(g, c0, c1, engine):
+            engine.tensor_tensor(
+                out=pair("L", g + 2)[:, 1, c0:c1, :],
+                in0=mix_w[g][:, :, c0:c1].rearrange("p t n -> p n t"),
+                in1=mix_h[g][:, :, c0:c1].rearrange("p t n -> p n t"),
+                op=ADD,
+            )
+
+        out_t = {}
+
+        def finish(g, s):
+            codes, scales = codes_t["L", g + 2]
+            acc = psum_m.tile([P, C], F32, name="acc")
+            nc.tensor.matmul_mx(
+                out=acc[:],
+                lhsT=codes[:, 1, P * s : P * (s + 1)].bitcast(FP8X4),
+                lhsT_scale=scales[:, 1, P * s : P * (s + 1)],
+                rhs=w_raw[:, 3, :].bitcast(FP4X4),
+                rhs_scale=s_raw[:, 3, :],
+                start=True,
+                stop=True,
+            )
+            if s % 2 == 0:
+                o = stream.tile([P, 2, C], F32, name="o", bufs=4)
+                out_t[0] = o
+            nc.vector.tensor_tensor(out=out_t[0][:, s % 2, :], in0=acc[:], in1=bias_p[:], op=ADD)
+            b, s0 = g // 2, 4 * (g % 2) + s
+            dst = out_rows[b].rearrange("(p s) c -> p s c", s=SLOTS)
+            if g == 7 and s >= 2:
+                nc.sync.dma_start(out=dst[:, s0, :], in_=out_t[0][:, s % 2, :])
+            elif s % 2 == 1:
+                nc.sync.dma_start(out=dst[:, s0 - 1 : s0 + 1, :], in_=out_t[0][:])
+
+        nc.vector.memset(s_raw[:].rearrange("p n c -> p (n c)").bitcast(I32), 0)
+        nc.vector.memset(warm[:], 0.0)
+        nc.scalar.dma_start(out=logits[:].rearrange("p b t k -> p b (t k)"), in_=a_logits.rearrange("b (p x) -> p b x", p=P))
+        nc.scalar.dma_start(out=yw_scale[:], in_=y_w_scale.rearrange("a o (p t) -> p (a o t)", p=P))
+        nc.scalar.dma_start(out=bias_h[:], in_=bo_h.rearrange("(p t) -> p t", p=P))
+        nc.scalar.dma_start(out=bias_w[:], in_=bo_w.rearrange("(p t) -> p t", p=P))
+        make_identity(nc, ident[:])
+        nc.vector.tensor_copy(
+            out=perm[:].rearrange("p (i q) -> p q i", q=4), in_=ident[:].rearrange("p (q i) -> p q i", q=4)
+        )
+        load_yh(0, 0, 4, nc.gpsimd)
+        load_yh(0, 4, 8, nc.gpsimd)
+        nc.gpsimd.dma_start(out=bias_p[:], in_=bp.partition_broadcast(P))
+        nc.scalar.activation(out=warm[:], in_=warm[:], func=ACT.Exp)
+
+        load_x(0, 0, 2)
+        load_yb(0, 0, 4)
+        load_x(0, 2, 4)
+        load_w(2, wc_words, wc_scales)
+        load_yb(0, 4, 8)
+        load_x(0, 4, 8)
+        load_w(1, ww_words, ww_scales)
+        load_w(0, wh_words, wh_scales)
+        load_x(1, 0, 8)
+        load_yb(1, 0, 8)
+        load_yh(1, 0, 8, nc.sync)
+        load_w(3, wp_words, wp_scales)
+
+        flat = "p b t k -> p (b t) k"
+        top_b = top[:].rearrange("p b t -> p (b t)").unsqueeze(2).to_broadcast([P, B * NT, 3])
+        total_b = total[:].rearrange("p b t -> p (b t)").unsqueeze(2).to_broadcast([P, B * NT, 3])
+        nc.vector.tensor_reduce(out=top[:].rearrange("p b t -> p (b t)"), in_=logits[:].rearrange(flat), axis=X_AXIS, op=MAX)
+        nc.vector.tensor_tensor(out=coef[:].rearrange(flat), in0=logits[:].rearrange(flat), in1=top_b, op=SUB)
+        nc.scalar.activation(
+            out=coef[:].rearrange("p b t k -> p (b t k)"), in_=coef[:].rearrange("p b t k -> p (b t k)"), func=ACT.Exp
+        )
+        nc.vector.tensor_reduce(out=total[:].rearrange("p b t -> p (b t)"), in_=coef[:].rearrange(flat), axis=X_AXIS, op=ADD)
+        nc.vector.reciprocal(out=total[:], in_=total[:])
+        nc.vector.tensor_tensor(out=coef[:].rearrange(flat), in0=coef[:].rearrange(flat), in1=total_b, op=MULT)
+        nc.vector.tensor_tensor(
+            out=beta[:], in0=coef[:, :, :, 0], in1=bias_h[:].unsqueeze(1).to_broadcast([P, B, NT]), op=MULT
+        )
+        nc.vector.tensor_tensor(
+            out=beta_w[:], in0=coef[:, :, :, 1], in1=bias_w[:].unsqueeze(1).to_broadcast([P, B, NT]), op=MULT
+        )
+        nc.vector.tensor_tensor(out=beta[:], in0=beta[:], in1=beta_w[:], op=ADD)
+        def bring(j, h_on_vector=False):
+            for which in ("w", "x", "h"):
+                transposes(j, which)
+            for which in ("w", "x", "h"):
+                evacuate(j, which, on_vector=h_on_vector and which == "h")
+
+        def branches(k, order=("x", "w", "h")):
+            g, half = k // 2, k % 2
+            for which in order:
+                for t in (2 * half, 2 * half + 1):
+                    mix(g, t, which, project(g, t, which, 0, C), 0, C)
+
+        def branches_by_tokens(k):
+            g, half = k // 2, k % 2
+            c0, c1 = 256 * half, 256 * half + 256
+            for tt in ((0, 1), (2, 3)):
+                for which in ("x", "w", "h"):
+                    for t in tt:
+                        mix(g, t, which, project(g, t, which, c0, c1), c0, c1)
+
+        def blend_pair(m, engines):
+            for i in range(2):
+                c0 = 256 * (m % 2) + 128 * i
+                blend(m // 2, c0, c0 + 128, engines[i])
+
+        def finish_pair(m):
+            finish(m // 2, 2 * (m % 2))
+            finish(m // 2, 2 * (m % 2) + 1)
+
+        def quantize_f(m):
+            c0 = 256 * (m % 2)
+            quantize("L", m // 2 + 2, 1, 2, c0, c0 + 256)
+
+        gg = (nc.gpsimd, nc.gpsimd)
+        gv = (nc.vector, nc.gpsimd)
+        vv = (nc.vector, nc.vector)
+        transposes(0, "x")
+        evacuate(0, "x")
+        permute_w(2)
+        cast_yw(0)
+        transposes(1, "x")
+        transposes(0, "w")
+        evacuate(1, "x")
+        evacuate(0, "w")
+        cast_yw(1)
+        transposes(0, "h")
+        evacuate(0, "h")
+        transposes(1, "w")
+        quantize("L", 0, 0, 1)
+        evacuate(1, "w")
+        transposes(1, "h")
+        evacuate(1, "h")
+        permute_w(1)
+        quantize("E", 0, 0, 1)
+        cast_yw(2)
+        permute_w(0)
+        quantize("E", 0, 1, 2)
+        transposes(2, "x")
+        branches(0, ("x",))
+        evacuate(2, "x")
+        transposes(2, "w")
+        cast_yw(3)
+        branches(0, ("w",))
+        evacuate(2, "w")
+        transposes(2, "h")
+        evacuate(2, "h", on_vector=True)
+        transposes(3, "w")
+        branches(0, ("h",))
+        evacuate(3, "w")
+        transposes(3, "x")
+        evacuate(3, "x")
+        transposes(3, "h")
+        cast_yw(4)
+        evacuate(3, "h", on_vector=True)
+        cast_yw(5)
+
+        for k in range(1, halves):
+            g, odd = k // 2, k % 2
+            if k == 1 or k == 5:
+                b = 2 if k == 1 else 3
+                load_x(b, 0, 8)
+                load_yb(b, 0, 8)
+                load_yh(b, 0, 8, nc.sync)
+            if odd and g + 1 < 8:
+                quantize("E", g + 1, 0, 2)
+            if not odd:
+                quantize("L", g, 0, 2 if g >= 2 else 1)
+            if k + 3 < halves:
+                bring(k + 3, h_on_vector=k < 4)
+            if k == 15:
+                quantize_f(12)
+            if k >= 4:
+                finish_pair(k - 4)
+            if k == 15:
+                finish_pair(12)
+            if k < 14:
+                branches(k)
+            else:
+                branches_by_tokens(k)
+            if k + 4 + CAST_MORE < halves:
+                cast_yw(k + 4 + CAST_MORE)
+            if g >= 1:
+                blend_pair(k - 2, gg)
+        quantize_f(13)
+        finish_pair(13)
+        blend_pair(14, vv)
+        quantize_f(14)
+        finish_pair(14)
+        blend_pair(15, gv)
+        quantize_f(15)
+        finish_pair(15)

@@ -23,6 +23,8 @@ P = 128
 SLOTS = 8
 NT = 4
 PAIR_BUFS = 3
+BLEND_CUTS = 4
+LATE_SHARE = 0
 CAST_MORE = 1
 CODE_BUFS = 3
 FLOPS = 2 * 4 * B * RES * RES * C * C
@@ -241,15 +243,15 @@ def tile_dynamixerblock_pb_w4_kernel(
 
         def blend(g, c0, c1, engine):
             engine.tensor_tensor(
-                out=pair("L", g + 2)[:, 1, c0:c1, :],
-                in0=mix_w[g][:, :, c0:c1].rearrange("p t n -> p n t"),
-                in1=mix_h[g][:, :, c0:c1].rearrange("p t n -> p n t"),
+                out=pair("L", g + 2)[:, 1, c0:c1, :].rearrange("p (c i) t -> p c t i", i=4),
+                in0=mix_w[g][:, :, c0:c1].rearrange("p t (c i) -> p c t i", i=4),
+                in1=mix_h[g][:, :, c0:c1].rearrange("p t (c i) -> p c t i", i=4),
                 op=ADD,
             )
 
         out_t = {}
 
-        def finish(g, s):
+        def finish(g, s, on_scalar=False):
             codes, scales = codes_t["L", g + 2]
             acc = psum_m.tile([P, C], F32, name="acc")
             nc.tensor.matmul_mx(
@@ -264,7 +266,12 @@ def tile_dynamixerblock_pb_w4_kernel(
             if s % 2 == 0:
                 o = stream.tile([P, 2, C], F32, name="o", bufs=4)
                 out_t[0] = o
-            nc.vector.tensor_tensor(out=out_t[0][:, s % 2, :], in0=acc[:], in1=bias_p[:], op=ADD)
+            if on_scalar:
+                plain = stream.tile([P, C], F32, name="plain", bufs=2)
+                nc.scalar.copy(out=plain[:], in_=acc[:])
+                nc.gpsimd.tensor_tensor(out=out_t[0][:, s % 2, :], in0=plain[:], in1=bias_p[:], op=ADD)
+            else:
+                nc.vector.tensor_tensor(out=out_t[0][:, s % 2, :], in0=acc[:], in1=bias_p[:], op=ADD)
             b, s0 = g // 2, 4 * (g % 2) + s
             dst = out_rows[b].rearrange("(p s) c -> p s c", s=SLOTS)
             if g == 7 and s >= 2:
@@ -339,19 +346,20 @@ def tile_dynamixerblock_pb_w4_kernel(
                         mix(g, t, which, project(g, t, which, c0, c1), c0, c1)
 
         def blend_pair(m, engines):
-            for i in range(2):
-                c0 = 256 * (m % 2) + 128 * i
-                blend(m // 2, c0, c0 + 128, engines[i])
+            step = 256 // len(engines)
+            for i in range(len(engines)):
+                c0 = 256 * (m % 2) + step * i
+                blend(m // 2, c0, c0 + step, engines[i])
 
-        def finish_pair(m):
-            finish(m // 2, 2 * (m % 2))
-            finish(m // 2, 2 * (m % 2) + 1)
+        def finish_pair(m, share=0):
+            finish(m // 2, 2 * (m % 2), share > 1)
+            finish(m // 2, 2 * (m % 2) + 1, share > 0)
 
         def quantize_f(m):
             c0 = 256 * (m % 2)
             quantize("L", m // 2 + 2, 1, 2, c0, c0 + 256)
 
-        gg = (nc.gpsimd, nc.gpsimd)
+        gg = (nc.gpsimd,) * BLEND_CUTS
         gv = (nc.vector, nc.gpsimd)
         vv = (nc.vector, nc.vector)
         transposes(0, "x")
@@ -404,15 +412,16 @@ def tile_dynamixerblock_pb_w4_kernel(
             if odd and g + 1 < 8:
                 quantize("E", g + 1, 0, 2)
             if not odd:
-                quantize("L", g, 0, 2 if g >= 2 else 1)
+                quantize("L", g, 0, 2 if 2 <= g < 7 else 1)
             if k + 3 < halves:
                 bring(k + 3, h_on_vector=k < 4)
+            if k >= 14:
+                quantize_f(k - 4)
+            if k >= 4:
+                finish_pair(k - 4, LATE_SHARE if k >= 13 else 0)
             if k == 15:
                 quantize_f(12)
-            if k >= 4:
-                finish_pair(k - 4)
-            if k == 15:
-                finish_pair(12)
+                finish_pair(12, LATE_SHARE)
             if k < 14:
                 branches(k)
             else:

@@ -243,9 +243,9 @@ def tile_dynamixerblock_pb_w4_kernel(
 
         def blend(g, c0, c1, engine):
             engine.tensor_tensor(
-                out=pair("L", g + 2)[:, 1, c0:c1, :].rearrange("p (c i) t -> p c t i", i=4),
-                in0=mix_w[g][:, :, c0:c1].rearrange("p t (c i) -> p c t i", i=4),
-                in1=mix_h[g][:, :, c0:c1].rearrange("p t (c i) -> p c t i", i=4),
+                out=pair("L", g + 2)[:, 1, c0:c1, :].rearrange("p (c i) t -> p c t i", i=2),
+                in0=mix_w[g][:, :, c0:c1].rearrange("p t (c i) -> p c t i", i=2),
+                in1=mix_h[g][:, :, c0:c1].rearrange("p t (c i) -> p c t i", i=2),
                 op=ADD,
             )
 

@@ -23,8 +23,15 @@ P = 128
 SLOTS = 8
 NT = 4
 PAIR_BUFS = 3
-BLEND_CUTS = 4
-LATE_SHARE = 0
+IL = "s"
+TIL = "ss"
+POS = 2
+MID = 1
+EARLY = 0
+MIDX = 0
+LATE = 1
+SH12 = 1
+TAILS = 0
 CAST_MORE = 1
 CODE_BUFS = 3
 FLOPS = 2 * 4 * B * RES * RES * C * C
@@ -211,43 +218,55 @@ def tile_dynamixerblock_pb_w4_kernel(
             return acc
 
         part = {}
+        plane_t = {}
 
         def mix(g, t, which, acc, c0, c1):
             b = g // 2
-            if g not in mix_h:
-                mh = stream.tile([P, NT, C], F32, name="mh")
-                mw = stream.tile([P, NT, C], F32, name="mw")
-                mix_h[g] = mh
-                mix_w[g] = mw
+            n = c1 - c0
             if which == "x":
                 part_c = stream.tile([P, C], F32, name="part_c", bufs=4)
-                part[t] = part_c
-                nc.scalar.activation(out=part_c[:, 0 : c1 - c0], in_=acc[:, 0 : c1 - c0], func=ACT.Copy, scale=coef[:, b, t, 2:3])
+                part["x", t] = part_c
+                nc.scalar.activation(
+                    out=part_c[:, 0:n],
+                    in_=acc[:, 0:n],
+                    func=ACT.Identity,
+                    bias=beta[:, b, t : t + 1],
+                    scale=coef[:, b, t, 2:3],
+                )
             elif which == "w":
+                part_w = stream.tile([P, C], F32, name="part_w", bufs=4)
+                part["w", t] = part_w
                 nc.vector.scalar_tensor_tensor(
-                    out=mix_w[g][:, t, c0:c1],
-                    in0=acc[:, 0 : c1 - c0],
+                    out=part_w[:, 0:n],
+                    in0=acc[:, 0:n],
                     scalar=coef[:, b, t, 1:2],
-                    in1=part[t][:, 0 : c1 - c0],
+                    in1=part["x", t][:, 0:n],
                     op0=MULT,
                     op1=ADD,
                 )
             else:
-                nc.scalar.activation(
-                    out=mix_h[g][:, t, c0:c1],
-                    in_=acc[:, 0 : c1 - c0],
-                    func=ACT.Identity,
-                    bias=beta[:, b, t : t + 1],
-                    scale=coef[:, b, t, 0:1],
+                if g not in plane_t:
+                    planes = stream.tile([P, NT, C], BF16, name="planes", bufs=3)
+                    plane_t[g] = planes
+                nc.vector.scalar_tensor_tensor(
+                    out=plane_t[g][:, t, c0:c1],
+                    in0=acc[:, 0:n],
+                    scalar=coef[:, b, t, 0:1],
+                    in1=part["w", t][:, 0:n],
+                    op0=MULT,
+                    op1=ADD,
                 )
 
-        def blend(g, c0, c1, engine):
-            engine.tensor_tensor(
-                out=pair("L", g + 2)[:, 1, c0:c1, :].rearrange("p (c i) t -> p c t i", i=2),
-                in0=mix_w[g][:, :, c0:c1].rearrange("p t (c i) -> p c t i", i=2),
-                in1=mix_h[g][:, :, c0:c1].rearrange("p t (c i) -> p c t i", i=2),
-                op=ADD,
-            )
+        def interleave(m, engine):
+            g, c0 = m // 2, 256 * (m % 2)
+            dst = pair("L", g + 2)[:, 1, c0 : c0 + 256, :].rearrange("p (c i) t -> p c t i", i=4)
+            src = plane_t[g][:, :, c0 : c0 + 256].rearrange("p t (c i) -> p c t i", i=4)
+            if engine == "v":
+                nc.vector.tensor_copy(out=dst, in_=src)
+            elif engine == "s":
+                nc.scalar.copy(out=dst, in_=src)
+            else:
+                nc.gpsimd.tensor_scalar(out=dst, in0=src, scalar1=1.0, scalar2=0.0, op0=MULT, op1=ADD)
 
         out_t = {}
 
@@ -337,19 +356,12 @@ def tile_dynamixerblock_pb_w4_kernel(
                 for t in (2 * half, 2 * half + 1):
                     mix(g, t, which, project(g, t, which, 0, C), 0, C)
 
-        def branches_by_tokens(k):
+        def branches_by_tokens(k, parts):
             g, half = k // 2, k % 2
             c0, c1 = 256 * half, 256 * half + 256
-            for tt in ((0, 1), (2, 3)):
-                for which in ("x", "w", "h"):
-                    for t in tt:
-                        mix(g, t, which, project(g, t, which, c0, c1), c0, c1)
-
-        def blend_pair(m, engines):
-            step = 256 // len(engines)
-            for i in range(len(engines)):
-                c0 = 256 * (m % 2) + step * i
-                blend(m // 2, c0, c0 + step, engines[i])
+            for tt, which in parts:
+                for t in tt:
+                    mix(g, t, which, project(g, t, which, c0, c1), c0, c1)
 
         def finish_pair(m, share=0):
             finish(m // 2, 2 * (m % 2), share > 1)
@@ -359,9 +371,6 @@ def tile_dynamixerblock_pb_w4_kernel(
             c0 = 256 * (m % 2)
             quantize("L", m // 2 + 2, 1, 2, c0, c0 + 256)
 
-        gg = (nc.gpsimd,) * BLEND_CUTS
-        gv = (nc.vector, nc.gpsimd)
-        vv = (nc.vector, nc.vector)
         transposes(0, "x")
         evacuate(0, "x")
         permute_w(2)
@@ -391,7 +400,7 @@ def tile_dynamixerblock_pb_w4_kernel(
         branches(0, ("w",))
         evacuate(2, "w")
         transposes(2, "h")
-        evacuate(2, "h", on_vector=True)
+        evacuate(2, "h")
         transposes(3, "w")
         branches(0, ("h",))
         evacuate(3, "w")
@@ -399,7 +408,7 @@ def tile_dynamixerblock_pb_w4_kernel(
         evacuate(3, "x")
         transposes(3, "h")
         cast_yw(4)
-        evacuate(3, "h", on_vector=True)
+        evacuate(3, "h")
         cast_yw(5)
 
         for k in range(1, halves):
@@ -414,27 +423,41 @@ def tile_dynamixerblock_pb_w4_kernel(
             if not odd:
                 quantize("L", g, 0, 2 if 2 <= g < 7 else 1)
             if k + 3 < halves:
-                bring(k + 3, h_on_vector=k < 4)
+                bring(k + 3, h_on_vector=k < EARLY)
             if k >= 14:
                 quantize_f(k - 4)
-            if k >= 4:
-                finish_pair(k - 4, LATE_SHARE if k >= 13 else 0)
             if k == 15:
                 quantize_f(12)
-                finish_pair(12, LATE_SHARE)
+            if g >= 1 and POS == 0:
+                interleave(k - 2, IL[k % len(IL)])
+            share = LATE if k >= 13 else MID + (k % 2) * MIDX
             if k < 14:
-                branches(k)
+                branches(k, ("x",))
             else:
-                branches_by_tokens(k)
-            if k + 4 + CAST_MORE < halves:
-                cast_yw(k + 4 + CAST_MORE)
-            if g >= 1:
-                blend_pair(k - 2, gg)
+                branches_by_tokens(k, (((0, 1), "x"),))
+            if k >= 4:
+                finish_pair(k - 4, share)
+            if k == 15:
+                finish_pair(12, SH12)
+            if g >= 1 and POS == 1:
+                interleave(k - 2, IL[k % len(IL)])
+            if k < 14:
+                branches(k, ("w", "h"))
+            else:
+                branches_by_tokens(
+                    k, (((0, 1), "w"), ((2, 3), "x"), ((0, 1), "h"), ((2, 3), "w"), ((2, 3), "h"))
+                )
+            if g >= 1 and POS == 2:
+                interleave(k - 2, IL[k % len(IL)])
+            if k + 5 < halves:
+                cast_yw(k + 5)
+            if g >= 1 and POS == 3:
+                interleave(k - 2, IL[k % len(IL)])
+        interleave(14, TIL[0])
         quantize_f(13)
-        finish_pair(13)
-        blend_pair(14, vv)
+        interleave(15, TIL[1])
+        finish_pair(13, TAILS)
         quantize_f(14)
-        finish_pair(14)
-        blend_pair(15, gv)
         quantize_f(15)
+        finish_pair(14, TAILS)
         finish_pair(15)

@@ -12,29 +12,27 @@ FP8 = mybir.dt.float8_e4m3fn
 FP8X4 = mybir.dt.float8_e4m3fn_x4
 FP4X4 = mybir.dt.float4_e2m1fn_x4
 ADD = mybir.AluOpType.add
-SUB = mybir.AluOpType.subtract
+SUBTRACT = mybir.AluOpType.subtract
 MULT = mybir.AluOpType.mult
 MAX = mybir.AluOpType.max
 ACT = mybir.ActivationFunctionType
 X_AXIS = mybir.AxisListType.X
 
-B, RES, C = 4, 32, 512
+IMAGES, RES, C = 4, 32, 512
 P = 128
-SLOTS = 8
 NT = 4
-PAIR_BUFS = 3
-IL = "s"
-TIL = "ss"
-POS = 2
-MID = 1
-EARLY = 0
-MIDX = 0
-LATE = 1
-SH12 = 1
-TAILS = 0
-CAST_MORE = 1
-CODE_BUFS = 3
-FLOPS = 2 * 4 * B * RES * RES * C * C
+SLOTS = RES * RES // P
+QUARTERS = RES // SLOTS
+STEP_SLOTS = 2
+STEP_COLS = STEP_SLOTS * P
+STEPS = IMAGES * SLOTS // STEP_SLOTS
+GROUPS = STEPS // 2
+GROUP_SLOTS = 2 * STEP_SLOTS
+F_LAG = 3
+FLOPS = 2 * 4 * IMAGES * RES * RES * C * C
+
+WH, WW, WC, WP = 0, 1, 2, 3
+BRANCH = {"x": ("L", 0, WC), "w": ("E", 0, WW), "h": ("E", 1, WH)}
 
 
 def tile_dynamixerblock_pb_w4_kernel(
@@ -44,420 +42,394 @@ def tile_dynamixerblock_pb_w4_kernel(
     y_w_scale,
     x,
     a_logits,
-    wh_words,
-    wh_scales,
+    wo_h_words,
+    wo_h_scales,
     bo_h,
-    ww_words,
-    ww_scales,
+    wo_w_words,
+    wo_w_scales,
     bo_w,
-    wc_words,
-    wc_scales,
+    wmlpc_words,
+    wmlpc_scales,
     wp_words,
     wp_scales,
     bp,
     out,
 ):
     nc = tc.nc
-    halves = 4 * B
     x_rows = x.rearrange("b i j c -> b (i j) c")
+    yw_rows = y_w_bytes.rearrange("(b i) j c -> b (i j) c", b=IMAGES)
     out_rows = out.rearrange("b i j c -> b (i j) c")
-    yw_rows = y_w_bytes.rearrange("(b i) j c -> b (i j) c", b=B)
 
     with ExitStack() as ctx:
         const = ctx.enter_context(tc.tile_pool(name="const", bufs=1))
-        stream = ctx.enter_context(tc.tile_pool(name="stream", bufs=2))
-        psum_t = ctx.enter_context(tc.psum_pool(name="psum_t", bufs=3))
-        psum_m = ctx.enter_context(tc.psum_pool(name="psum_m", bufs=5))
+        stream = ctx.enter_context(tc.tile_pool(name="stream", bufs=3))
+        psum = ctx.enter_context(tc.psum_pool(name="psum", bufs=8))
         ctx.enter_context(tc.manual_schedule())
 
         ident = const.tile([P, P], F32, name="ident")
-        perm = const.tile([P, P], F32, name="perm")
+        regroup = const.tile([P, P], F32, name="regroup")
         warm = const.tile([P, 1], F32, name="warm")
         w_raw = const.tile([P, 4, 2 * C], U8, name="w_raw", align_bytes=64)
         s_raw = const.tile([P, 4, C], U8, name="s_raw", align_bytes=64)
         w_perm = const.tile([P, 3, 2 * C], U8, name="w_perm", align_bytes=64)
         s_perm = const.tile([P, 3, C], U8, name="s_perm", align_bytes=64)
-        logits = const.tile([P, B, NT, 3], BF16, name="logits")
-        top = const.tile([P, B, NT], F32, name="top")
-        total = const.tile([P, B, NT], F32, name="total")
-        coef = const.tile([P, B, NT, 3], F32, name="coef")
-        beta = const.tile([P, B, NT], F32, name="beta")
-        beta_w = const.tile([P, B, NT], F32, name="beta_w")
+        logits = const.tile([P, IMAGES, NT, 3], BF16, name="logits")
+        top = const.tile([P, IMAGES, NT], F32, name="top")
+        total = const.tile([P, IMAGES, NT], F32, name="total")
+        coef = const.tile([P, IMAGES, NT, 3], F32, name="coef")
+        beta = const.tile([P, IMAGES, NT], F32, name="beta")
+        beta_w = const.tile([P, IMAGES, NT], F32, name="beta_w")
         bias_h = const.tile([P, NT], BF16, name="bias_h")
         bias_w = const.tile([P, NT], BF16, name="bias_w")
         bias_p = const.tile([P, C], BF16, name="bias_p")
-        yw_scale = const.tile([P, NT], F32, name="yw_scale")
-        x_sb = []
-        yh_sb = []
-        yb_sb = []
-        for b in range(B):
+        yw_scale = const.tile([P, STEP_SLOTS, C], F32, name="yw_scale")
+        x_sb, yh_sb, yw_sb = [], [], []
+        for b in range(IMAGES):
             x_b = const.tile([P, SLOTS, C], BF16, name="x_sb%d" % b)
             yh_b = const.tile([P, SLOTS, C], BF16, name="yh_sb%d" % b)
-            yb_b = const.tile([P, SLOTS, C], U8, name="yb_sb%d" % b)
+            yw_b = const.tile([P, SLOTS, C], U8, name="yw_sb%d" % b)
             x_sb.append(x_b)
             yh_sb.append(yh_b)
-            yb_sb.append(yb_b)
+            yw_sb.append(yw_b)
 
         def load_x(b, s0, s1):
-            nc.sync.dma_start(out=x_sb[b][:, s0:s1, :], in_=x_rows[b].rearrange("(p s) c -> p s c", s=SLOTS)[:, s0:s1, :])
+            nc.sync.dma_start(
+                out=x_sb[b][:, s0:s1, :], in_=x_rows[b].rearrange("(p s) c -> p s c", s=SLOTS)[:, s0:s1, :]
+            )
 
-        def load_yb(b, s0, s1):
-            nc.sync.dma_start(out=yb_sb[b][:, s0:s1, :], in_=yw_rows[b].rearrange("(p s) c -> p s c", s=SLOTS)[:, s0:s1, :])
+        def load_yw(b, s0, s1):
+            nc.sync.dma_start(
+                out=yw_sb[b][:, s0:s1, :], in_=yw_rows[b].rearrange("(p s) c -> p s c", s=SLOTS)[:, s0:s1, :]
+            )
 
         def load_yh(b, s0, s1, queue):
-            for jq in range(4):
-                r0 = b * RES + SLOTS * jq
+            for q in range(QUARTERS):
+                first = b * RES + SLOTS * q
                 queue.dma_start(
-                    out=yh_sb[b][32 * jq : 32 * jq + 32, s0:s1, :],
-                    in_=y_h[r0 + s0 : r0 + s1].rearrange("s i c -> i s c"),
+                    out=yh_sb[b][RES * q : RES * (q + 1), s0:s1, :],
+                    in_=y_h[first + s0 : first + s1].rearrange("s i c -> i s c"),
                 )
 
-        def load_w(n, words, scales):
+        def load_image(b):
+            load_x(b, 0, SLOTS)
+            load_yw(b, 0, SLOTS)
+            load_yh(b, 0, SLOTS, nc.sync)
+
+        def load_words(n, words):
             nc.sync.dma_start(out=w_raw[:, n, :], in_=words[0])
+
+        def load_scales(n, scales):
             for q in range(4):
                 nc.sync.dma_start(
-                    out=s_raw[32 * q : 32 * q + 4, n, :].bitcast(I32),
-                    in_=scales[0, 4 * q : 4 * q + 4, :].bitcast(I32),
+                    out=s_raw[32 * q : 32 * q + 4, n, :].bitcast(I32), in_=scales[0, 4 * q : 4 * q + 4, :].bitcast(I32)
                 )
 
-        def permute_w(n):
+        def permute_words(n):
             nc.vector.tensor_copy(
                 out=w_perm[:, n, :].rearrange("p (t m e) -> p t m e", t=NT, e=2),
                 in_=w_raw[:, n, :].rearrange("p (m t e) -> p t m e", t=NT, e=2),
             )
+
+        def permute_scales(n):
             nc.vector.tensor_copy(
                 out=s_perm[:, n, :].rearrange("p (t m) -> p t m", t=NT),
                 in_=s_raw[:, n, :].rearrange("p (m t) -> p t m", t=NT),
             )
 
-        cast_t = {}
-        bank_t = {}
-        pair_t = {}
-        codes_t = {}
-        mix_h = {}
-        mix_w = {}
+        wide, turned, pairs, codes_of = {}, {}, {}, {}
 
-        def cast_yw(k):
-            b, s0 = k // 4, 2 * (k % 4)
-            yw = stream.tile([P, 2, C], BF16, name="yw_cast", bufs=4)
-            nc.scalar.activation(
+        def place(k):
+            return divmod(k * STEP_SLOTS, SLOTS)
+
+        def widen_yw(k):
+            b, s0 = place(k)
+            yw = stream.tile([P, STEP_SLOTS, C], BF16, name="yw_wide")
+            nc.vector.tensor_tensor(
                 out=yw[:].rearrange("p s c -> p (s c)"),
-                in_=yb_sb[b][:, s0 : s0 + 2, :].rearrange("p s c -> p (s c)").bitcast(FP8),
-                func=ACT.Copy,
+                in0=yw_sb[b][:, s0 : s0 + STEP_SLOTS, :].rearrange("p s c -> p (s c)").bitcast(FP8),
+                in1=yw_scale[:].rearrange("p s c -> p (s c)"),
+                op=MULT,
             )
-            cast_t[k] = yw
+            wide[k] = yw
 
-        def transposes(k, which):
-            b, s0 = k // 4, 2 * (k % 4)
-            if which == "x":
-                src = x_sb[b][:, s0 : s0 + 2, :]
-            elif which == "h":
-                src = yh_sb[b][:, s0 : s0 + 2, :]
-            else:
-                src = cast_t[k][:]
-            bank = psum_t.tile([P, 2, 2, P], F32, name="bank")
-            for s in range(2):
+        def turn(k, branch):
+            b, s0 = place(k)
+            src = {"x": x_sb[b], "h": yh_sb[b]}[branch][:, s0 : s0 + STEP_SLOTS, :] if branch != "w" else wide.pop(k)[:]
+            bank = psum.tile([P, 2, STEP_SLOTS, P], F32, name="bank", tag="bank")
+            for s in range(STEP_SLOTS):
                 words = src[:, s, :].bitcast(F32)
                 for u in range(2):
-                    nc.tensor.transpose(bank[:, u, s, :], words[:, u : 2 * P : 2], perm[:] if which == "h" else ident[:])
-            bank_t[k, which] = bank
+                    nc.tensor.transpose(
+                        bank[:, u, s, :], words[:, u : C // 2 : 2], regroup[:] if branch == "h" else ident[:]
+                    )
+            turned[k, branch] = bank
 
         def pair(name, g):
-            if (name, g) not in pair_t:
-                tile = stream.tile([P, 2, C, NT], BF16, name="pair_" + name, align_bytes=64, bufs=PAIR_BUFS)
-                pair_t[name, g] = tile
-            return pair_t[name, g]
+            if (name, g) not in pairs:
+                operands = stream.tile([P, 2, C, NT], BF16, name="pair_" + name, align_bytes=64)
+                pairs[name, g] = operands
+            return pairs[name, g]
 
-        def evacuate(k, which, on_vector=False):
-            bank = bank_t.pop((k, which))
-            g, half = k // 2, k % 2
-            cols = slice(2 * P * half, 2 * P * (half + 1))
-            if which == "w":
-                nc.vector.tensor_tensor(
-                    out=pair("E", g)[:, 0, cols, :].rearrange("p n (u e) -> p n u e", e=2),
-                    in0=bank[:].rearrange("p u s r -> p (u s r)").bitcast(BF16).rearrange("p (u n e) -> p n u e", u=2, e=2),
-                    in1=yw_scale[:].rearrange("p (u e) -> p u e", e=2).unsqueeze(1).to_broadcast([P, 2 * P, 2, 2]),
-                    op=MULT,
-                )
-            else:
-                dst = pair("L", g)[:, 0, cols, :] if which == "x" else pair("E", g)[:, 1, cols, :]
-                dst = dst.rearrange("p n t -> p (n t)").bitcast(F32).rearrange("p (n u) -> p n u", u=2)
-                words = bank[:].rearrange("p u s r -> p (s r) u")
-                if on_vector:
-                    nc.vector.tensor_copy(out=dst, in_=words)
-                else:
-                    nc.scalar.copy(out=dst, in_=words)
+        def group_cols(k):
+            return slice(STEP_COLS * (k % 2), STEP_COLS * (k % 2 + 1))
 
-        def quantize(name, g, i0, i1, c0=0, c1=C):
-            if (name, g) not in codes_t:
-                codes = stream.tile([P, 2, C], U32, name="codes_" + name, align_bytes=64, bufs=CODE_BUFS)
-                scales = stream.tile([P, 2, C], U8, name="scales_" + name, align_bytes=64, bufs=CODE_BUFS)
-                codes_t[name, g] = (codes, scales)
-            codes, scales = codes_t[name, g]
-            nc.vector.quantize_mx(
-                out=codes[:, i0:i1, c0:c1].rearrange("p i c -> p (i c)").bitcast(FP8X4),
-                scales=scales[:, i0:i1, c0:c1].rearrange("p i c -> p (i c)"),
-                in_=pair(name, g)[:, i0:i1, c0:c1, :].rearrange("p i n t -> p (i n t)"),
+        def collect(k, branch):
+            name, i, n = BRANCH[branch]
+            dst = pair(name, k // 2)[:, i, group_cols(k), :].rearrange("p n t -> p (n t)").bitcast(F32)
+            nc.scalar.copy(
+                out=dst.rearrange("p (n u) -> p n u", u=2), in_=turned.pop((k, branch))[:].rearrange("p u s r -> p (s r) u")
             )
 
-        OPERAND = {"x": ("L", 0, 2), "w": ("E", 0, 1), "h": ("E", 1, 0)}
+        def bring(k, branch):
+            turn(k, branch)
+            collect(k, branch)
 
-        def project(g, t, which, c0, c1):
-            name, i, n = OPERAND[which]
-            codes, scales = codes_t[name, g]
-            acc = psum_m.tile([P, C], F32, name="acc")
+        def quantize(name, g, i0, i1, cols=slice(0, C)):
+            if (name, g) not in codes_of:
+                codes = stream.tile([P, 2, C], U32, name="codes_" + name, align_bytes=64)
+                scales = stream.tile([P, 2, C], U8, name="scales_" + name, align_bytes=64)
+                codes_of[name, g] = (codes, scales)
+            codes, scales = codes_of[name, g]
+            nc.vector.quantize_mx(
+                out=codes[:, i0:i1, cols].rearrange("p i c -> p (i c)").bitcast(FP8X4),
+                scales=scales[:, i0:i1, cols].rearrange("p i c -> p (i c)"),
+                in_=pair(name, g)[:, i0:i1, cols, :].rearrange("p i n t -> p (i n t)"),
+            )
+
+        def quantize_f(k):
+            quantize("L", k // 2 + F_LAG, 1, 2, group_cols(k))
+
+        partial, planes = {}, {}
+
+        def project(g, t, branch, cols):
+            name, i, n = BRANCH[branch]
+            codes, scales = codes_of[name, g]
+            acc = psum.tile([P, C], F32, name="acc", tag="bank")
             nc.tensor.matmul_mx(
-                out=acc[:, 0 : c1 - c0],
+                out=acc[:, 0 : cols.stop - cols.start],
                 lhsT=w_perm[:, n, 2 * P * t : 2 * P * (t + 1)].bitcast(FP4X4),
                 lhsT_scale=s_perm[:, n, P * t : P * (t + 1)],
-                rhs=codes[:, i, c0:c1].bitcast(FP8X4),
-                rhs_scale=scales[:, i, c0:c1],
+                rhs=codes[:, i, cols].bitcast(FP8X4),
+                rhs_scale=scales[:, i, cols],
                 start=True,
                 stop=True,
             )
             return acc
 
-        part = {}
-        plane_t = {}
-
-        def mix(g, t, which, acc, c0, c1):
-            b = g // 2
-            n = c1 - c0
-            if which == "x":
-                part_c = stream.tile([P, C], F32, name="part_c", bufs=4)
-                part["x", t] = part_c
+        def add_branch(g, t, branch, cols):
+            b = g * GROUP_SLOTS // SLOTS
+            width = cols.stop - cols.start
+            acc = project(g, t, branch, cols)[:, 0:width]
+            if branch == "x":
+                c_part = stream.tile([P, C], F32, name="c_part", bufs=4)
+                partial[t] = c_part
                 nc.scalar.activation(
-                    out=part_c[:, 0:n],
-                    in_=acc[:, 0:n],
+                    out=c_part[:, 0:width],
+                    in_=acc,
                     func=ACT.Identity,
                     bias=beta[:, b, t : t + 1],
                     scale=coef[:, b, t, 2:3],
                 )
-            elif which == "w":
-                part_w = stream.tile([P, C], F32, name="part_w", bufs=4)
-                part["w", t] = part_w
-                nc.vector.scalar_tensor_tensor(
-                    out=part_w[:, 0:n],
-                    in0=acc[:, 0:n],
-                    scalar=coef[:, b, t, 1:2],
-                    in1=part["x", t][:, 0:n],
-                    op0=MULT,
-                    op1=ADD,
-                )
+                return
+            if branch == "w":
+                cw_part = stream.tile([P, C], F32, name="cw_part", bufs=4)
+                dst, a = cw_part[:, 0:width], coef[:, b, t, 1:2]
             else:
-                if g not in plane_t:
-                    planes = stream.tile([P, NT, C], BF16, name="planes", bufs=3)
-                    plane_t[g] = planes
-                nc.vector.scalar_tensor_tensor(
-                    out=plane_t[g][:, t, c0:c1],
-                    in0=acc[:, 0:n],
-                    scalar=coef[:, b, t, 0:1],
-                    in1=part["w", t][:, 0:n],
-                    op0=MULT,
-                    op1=ADD,
-                )
-
-        def interleave(m, engine):
-            g, c0 = m // 2, 256 * (m % 2)
-            dst = pair("L", g + 2)[:, 1, c0 : c0 + 256, :].rearrange("p (c i) t -> p c t i", i=4)
-            src = plane_t[g][:, :, c0 : c0 + 256].rearrange("p t (c i) -> p c t i", i=4)
-            if engine == "v":
-                nc.vector.tensor_copy(out=dst, in_=src)
-            elif engine == "s":
-                nc.scalar.copy(out=dst, in_=src)
-            else:
-                nc.gpsimd.tensor_scalar(out=dst, in0=src, scalar1=1.0, scalar2=0.0, op0=MULT, op1=ADD)
-
-        out_t = {}
-
-        def finish(g, s, on_scalar=False):
-            codes, scales = codes_t["L", g + 2]
-            acc = psum_m.tile([P, C], F32, name="acc")
-            nc.tensor.matmul_mx(
-                out=acc[:],
-                lhsT=codes[:, 1, P * s : P * (s + 1)].bitcast(FP8X4),
-                lhsT_scale=scales[:, 1, P * s : P * (s + 1)],
-                rhs=w_raw[:, 3, :].bitcast(FP4X4),
-                rhs_scale=s_raw[:, 3, :],
-                start=True,
-                stop=True,
+                if g not in planes:
+                    f_planes = stream.tile([P, NT, C], BF16, name="f_planes")
+                    planes[g] = f_planes
+                dst, a = planes[g][:, t, cols], coef[:, b, t, 0:1]
+            nc.vector.scalar_tensor_tensor(
+                out=dst, in0=acc, scalar=a, in1=partial[t][:, 0:width], op0=MULT, op1=ADD
             )
-            if s % 2 == 0:
-                o = stream.tile([P, 2, C], F32, name="o", bufs=4)
-                out_t[0] = o
-            if on_scalar:
-                plain = stream.tile([P, C], F32, name="plain", bufs=2)
-                nc.scalar.copy(out=plain[:], in_=acc[:])
-                nc.gpsimd.tensor_tensor(out=out_t[0][:, s % 2, :], in0=plain[:], in1=bias_p[:], op=ADD)
-            else:
-                nc.vector.tensor_tensor(out=out_t[0][:, s % 2, :], in0=acc[:], in1=bias_p[:], op=ADD)
-            b, s0 = g // 2, 4 * (g % 2) + s
+            if branch == "w":
+                partial[t] = cw_part
+
+        def add_branches(k, branches):
+            for branch in branches:
+                for t in (2 * (k % 2), 2 * (k % 2) + 1):
+                    add_branch(k // 2, t, branch, slice(0, C))
+
+        def interleave(k):
+            cols = group_cols(k)
+            nc.scalar.copy(
+                out=pair("L", k // 2 + F_LAG)[:, 1, cols, :].rearrange("p (n r) t -> p n t r", r=4),
+                in_=planes[k // 2][:, :, cols].rearrange("p t (n r) -> p n t r", r=4),
+            )
+
+        def project_out(k, share):
+            b, s0 = place(k)
+            codes, scales = codes_of["L", k // 2 + F_LAG]
+            o = stream.tile([P, STEP_SLOTS, C], F32, name="o", bufs=4)
             dst = out_rows[b].rearrange("(p s) c -> p s c", s=SLOTS)
-            if g == 7 and s >= 2:
-                nc.sync.dma_start(out=dst[:, s0, :], in_=out_t[0][:, s % 2, :])
-            elif s % 2 == 1:
-                nc.sync.dma_start(out=dst[:, s0 - 1 : s0 + 1, :], in_=out_t[0][:])
+            for s in range(STEP_SLOTS):
+                tokens = slice(STEP_COLS * (k % 2) + P * s, STEP_COLS * (k % 2) + P * (s + 1))
+                acc = psum.tile([P, C], F32, name="acc", tag="bank")
+                nc.tensor.matmul_mx(
+                    out=acc[:],
+                    lhsT=codes[:, 1, tokens].bitcast(FP8X4),
+                    lhsT_scale=scales[:, 1, tokens],
+                    rhs=w_raw[:, WP, :].bitcast(FP4X4),
+                    rhs_scale=s_raw[:, WP, :],
+                    start=True,
+                    stop=True,
+                )
+                if share and s == 1:
+                    plain = stream.tile([P, C], F32, name="plain")
+                    nc.scalar.copy(out=plain[:], in_=acc[:])
+                    nc.gpsimd.tensor_tensor(out=o[:, s, :], in0=plain[:], in1=bias_p[:], op=ADD)
+                else:
+                    nc.vector.tensor_tensor(out=o[:, s, :], in0=acc[:], in1=bias_p[:], op=ADD)
+                if k == STEPS - 1:
+                    nc.sync.dma_start(out=dst[:, s0 + s, :], in_=o[:, s, :])
+            if k < STEPS - 1:
+                nc.sync.dma_start(out=dst[:, s0 : s0 + STEP_SLOTS, :], in_=o[:])
 
         nc.vector.memset(s_raw[:].rearrange("p n c -> p (n c)").bitcast(I32), 0)
         nc.vector.memset(warm[:], 0.0)
-        nc.scalar.dma_start(out=logits[:].rearrange("p b t k -> p b (t k)"), in_=a_logits.rearrange("b (p x) -> p b x", p=P))
-        nc.scalar.dma_start(out=yw_scale[:], in_=y_w_scale.rearrange("a o (p t) -> p (a o t)", p=P))
+        nc.scalar.dma_start(
+            out=logits[:].rearrange("p b t k -> p b (t k)"), in_=a_logits.rearrange("b (p x) -> p b x", p=P)
+        )
+        nc.scalar.dma_start(out=yw_scale[:, 0, :], in_=y_w_scale.rearrange("a o c -> (a o c)").partition_broadcast(P))
         nc.scalar.dma_start(out=bias_h[:], in_=bo_h.rearrange("(p t) -> p t", p=P))
         nc.scalar.dma_start(out=bias_w[:], in_=bo_w.rearrange("(p t) -> p t", p=P))
+        nc.scalar.activation(out=warm[:], in_=warm[:], func=ACT.Exp)
         make_identity(nc, ident[:])
         nc.vector.tensor_copy(
-            out=perm[:].rearrange("p (i q) -> p q i", q=4), in_=ident[:].rearrange("p (q i) -> p q i", q=4)
+            out=regroup[:].rearrange("p (i q) -> p q i", q=QUARTERS), in_=ident[:].rearrange("p (q i) -> p q i", q=QUARTERS)
         )
-        load_yh(0, 0, 4, nc.gpsimd)
-        load_yh(0, 4, 8, nc.gpsimd)
+        load_yh(0, 0, GROUP_SLOTS, nc.gpsimd)
+        load_yh(0, GROUP_SLOTS, SLOTS, nc.gpsimd)
         nc.gpsimd.dma_start(out=bias_p[:], in_=bp.partition_broadcast(P))
-        nc.scalar.activation(out=warm[:], in_=warm[:], func=ACT.Exp)
-
+        load_scales(WC, wmlpc_scales)
         load_x(0, 0, 2)
-        load_yb(0, 0, 4)
+        load_yw(0, 0, 4)
+        load_words(WC, wmlpc_words)
         load_x(0, 2, 4)
-        load_w(2, wc_words, wc_scales)
-        load_yb(0, 4, 8)
+        load_scales(WW, wo_w_scales)
+        load_scales(WH, wo_h_scales)
+        load_words(WW, wo_w_words)
+        load_words(WH, wo_h_words)
+        load_yw(0, 4, 8)
         load_x(0, 4, 8)
-        load_w(1, ww_words, ww_scales)
-        load_w(0, wh_words, wh_scales)
-        load_x(1, 0, 8)
-        load_yb(1, 0, 8)
-        load_yh(1, 0, 8, nc.sync)
-        load_w(3, wp_words, wp_scales)
-
+        load_image(1)
+        load_scales(WP, wp_scales)
+        load_words(WP, wp_words)
         flat = "p b t k -> p (b t) k"
-        top_b = top[:].rearrange("p b t -> p (b t)").unsqueeze(2).to_broadcast([P, B * NT, 3])
-        total_b = total[:].rearrange("p b t -> p (b t)").unsqueeze(2).to_broadcast([P, B * NT, 3])
-        nc.vector.tensor_reduce(out=top[:].rearrange("p b t -> p (b t)"), in_=logits[:].rearrange(flat), axis=X_AXIS, op=MAX)
-        nc.vector.tensor_tensor(out=coef[:].rearrange(flat), in0=logits[:].rearrange(flat), in1=top_b, op=SUB)
+        top_b = top[:].rearrange("p b t -> p (b t)").unsqueeze(2).to_broadcast([P, IMAGES * NT, 3])
+        total_b = total[:].rearrange("p b t -> p (b t)").unsqueeze(2).to_broadcast([P, IMAGES * NT, 3])
+        nc.vector.tensor_reduce(
+            out=top[:].rearrange("p b t -> p (b t)"), in_=logits[:].rearrange(flat), axis=X_AXIS, op=MAX
+        )
+        nc.vector.tensor_tensor(out=coef[:].rearrange(flat), in0=logits[:].rearrange(flat), in1=top_b, op=SUBTRACT)
         nc.scalar.activation(
             out=coef[:].rearrange("p b t k -> p (b t k)"), in_=coef[:].rearrange("p b t k -> p (b t k)"), func=ACT.Exp
         )
-        nc.vector.tensor_reduce(out=total[:].rearrange("p b t -> p (b t)"), in_=coef[:].rearrange(flat), axis=X_AXIS, op=ADD)
+        nc.vector.tensor_reduce(
+            out=total[:].rearrange("p b t -> p (b t)"), in_=coef[:].rearrange(flat), axis=X_AXIS, op=ADD
+        )
         nc.vector.reciprocal(out=total[:], in_=total[:])
         nc.vector.tensor_tensor(out=coef[:].rearrange(flat), in0=coef[:].rearrange(flat), in1=total_b, op=MULT)
         nc.vector.tensor_tensor(
-            out=beta[:], in0=coef[:, :, :, 0], in1=bias_h[:].unsqueeze(1).to_broadcast([P, B, NT]), op=MULT
+            out=beta[:], in0=coef[:, :, :, 0], in1=bias_h[:].unsqueeze(1).to_broadcast([P, IMAGES, NT]), op=MULT
         )
         nc.vector.tensor_tensor(
-            out=beta_w[:], in0=coef[:, :, :, 1], in1=bias_w[:].unsqueeze(1).to_broadcast([P, B, NT]), op=MULT
+            out=beta_w[:], in0=coef[:, :, :, 1], in1=bias_w[:].unsqueeze(1).to_broadcast([P, IMAGES, NT]), op=MULT
         )
         nc.vector.tensor_tensor(out=beta[:], in0=beta[:], in1=beta_w[:], op=ADD)
-        def bring(j, h_on_vector=False):
-            for which in ("w", "x", "h"):
-                transposes(j, which)
-            for which in ("w", "x", "h"):
-                evacuate(j, which, on_vector=h_on_vector and which == "h")
+        nc.scalar.copy(out=yw_scale[:, 1, :], in_=yw_scale[:, 0, :])
 
-        def branches(k, order=("x", "w", "h")):
-            g, half = k // 2, k % 2
-            for which in order:
-                for t in (2 * half, 2 * half + 1):
-                    mix(g, t, which, project(g, t, which, 0, C), 0, C)
-
-        def branches_by_tokens(k, parts):
-            g, half = k // 2, k % 2
-            c0, c1 = 256 * half, 256 * half + 256
-            for tt, which in parts:
-                for t in tt:
-                    mix(g, t, which, project(g, t, which, c0, c1), c0, c1)
-
-        def finish_pair(m, share=0):
-            finish(m // 2, 2 * (m % 2), share > 1)
-            finish(m // 2, 2 * (m % 2) + 1, share > 0)
-
-        def quantize_f(m):
-            c0 = 256 * (m % 2)
-            quantize("L", m // 2 + 2, 1, 2, c0, c0 + 256)
-
-        transposes(0, "x")
-        evacuate(0, "x")
-        permute_w(2)
-        cast_yw(0)
-        transposes(1, "x")
-        transposes(0, "w")
-        evacuate(1, "x")
-        evacuate(0, "w")
-        cast_yw(1)
-        transposes(0, "h")
-        evacuate(0, "h")
-        transposes(1, "w")
+        bring(0, "x")
+        widen_yw(0)
+        permute_words(WC)
+        permute_scales(WC)
+        bring(0, "w")
+        bring(1, "x")
+        widen_yw(1)
+        bring(0, "h")
+        bring(1, "w")
         quantize("L", 0, 0, 1)
-        evacuate(1, "w")
-        transposes(1, "h")
-        evacuate(1, "h")
-        permute_w(1)
+        bring(1, "h")
+        permute_words(WW)
+        permute_scales(WW)
         quantize("E", 0, 0, 1)
-        cast_yw(2)
-        permute_w(0)
+        add_branches(0, "x")
+        bring(2, "x")
+        permute_words(WH)
+        permute_scales(WH)
         quantize("E", 0, 1, 2)
-        transposes(2, "x")
-        branches(0, ("x",))
-        evacuate(2, "x")
-        transposes(2, "w")
-        cast_yw(3)
-        branches(0, ("w",))
-        evacuate(2, "w")
-        transposes(2, "h")
-        evacuate(2, "h")
-        transposes(3, "w")
-        branches(0, ("h",))
-        evacuate(3, "w")
-        transposes(3, "x")
-        evacuate(3, "x")
-        transposes(3, "h")
-        cast_yw(4)
-        evacuate(3, "h")
-        cast_yw(5)
-
-        for k in range(1, halves):
+        widen_yw(2)
+        add_branches(0, "w")
+        bring(2, "h")
+        add_branches(0, "h")
+        add_branches(1, "x")
+        turn(2, "w")
+        turn(3, "x")
+        collect(2, "w")
+        collect(3, "x")
+        widen_yw(3)
+        add_branches(1, "w")
+        bring(3, "h")
+        add_branches(1, "h")
+        bring(3, "w")
+        load_image(2)
+        widen_yw(4)
+        quantize("L", 1, 0, 1)
+        quantize("E", 1, 0, 2)
+        for branch in "xhw":
+            turn(4, branch)
+        for branch in "xhw":
+            collect(4, branch)
+        widen_yw(5)
+        for k in range(2, STEPS - 2):
             g, odd = k // 2, k % 2
-            if k == 1 or k == 5:
-                b = 2 if k == 1 else 3
-                load_x(b, 0, 8)
-                load_yb(b, 0, 8)
-                load_yh(b, 0, 8, nc.sync)
-            if odd and g + 1 < 8:
+            if k == 5:
+                load_image(3)
+            if odd and g + 1 < GROUPS:
+                quantize("L", g + 1, 0, 2 if g + 1 >= F_LAG else 1)
                 quantize("E", g + 1, 0, 2)
-            if not odd:
-                quantize("L", g, 0, 2 if 2 <= g < 7 else 1)
-            if k + 3 < halves:
-                bring(k + 3, h_on_vector=k < EARLY)
-            if k >= 14:
-                quantize_f(k - 4)
-            if k == 15:
-                quantize_f(12)
-            if g >= 1 and POS == 0:
-                interleave(k - 2, IL[k % len(IL)])
-            share = LATE if k >= 13 else MID + (k % 2) * MIDX
-            if k < 14:
-                branches(k, ("x",))
-            else:
-                branches_by_tokens(k, (((0, 1), "x"),))
-            if k >= 4:
-                finish_pair(k - 4, share)
-            if k == 15:
-                finish_pair(12, SH12)
-            if g >= 1 and POS == 1:
-                interleave(k - 2, IL[k % len(IL)])
-            if k < 14:
-                branches(k, ("w", "h"))
-            else:
-                branches_by_tokens(
-                    k, (((0, 1), "w"), ((2, 3), "x"), ((0, 1), "h"), ((2, 3), "w"), ((2, 3), "h"))
-                )
-            if g >= 1 and POS == 2:
-                interleave(k - 2, IL[k % len(IL)])
-            if k + 5 < halves:
-                cast_yw(k + 5)
-            if g >= 1 and POS == 3:
-                interleave(k - 2, IL[k % len(IL)])
-        interleave(14, TIL[0])
-        quantize_f(13)
-        interleave(15, TIL[1])
-        finish_pair(13, TAILS)
-        quantize_f(14)
-        quantize_f(15)
-        finish_pair(14, TAILS)
-        finish_pair(15)
+            if k == 2:
+                add_branches(k, "x")
+            if k + 4 < STEPS:
+                widen_yw(k + 4)
+            if k + 3 < STEPS:
+                for branch in "xhw":
+                    turn(k + 3, branch)
+                for branch in "xhw":
+                    collect(k + 3, branch)
+            if k > 2:
+                add_branches(k, "x")
+            if k >= 5:
+                project_out(k - 5, share=True)
+            add_branches(k, "wh")
+            interleave(k - 2)
+
+        for k in (STEPS - 2, STEPS - 1):
+            def half(branch, *tiles):
+                for t in tiles:
+                    add_branch(GROUPS - 1, t, branch, group_cols(k))
+
+            quantize_f(k - 4)
+            if k == STEPS - 1:
+                quantize_f(k - 3)
+            half("x", 0, 1)
+            if k == STEPS - 2:
+                project_out(k - 5, share=True)
+            project_out(k - 4, share=True)
+            if k == STEPS - 1:
+                project_out(k - 3, share=True)
+            half("w", 0, 1)
+            half("x", 2, 3)
+            half("h", 0, 1)
+            half("w", 2, 3)
+            half("h", 2, 3)
+            interleave(k - 2)
+
+        interleave(STEPS - 2)
+        quantize_f(STEPS - 3)
+        interleave(STEPS - 1)
+        project_out(STEPS - 3, share=False)
+        quantize_f(STEPS - 2)
+        quantize_f(STEPS - 1)
+        project_out(STEPS - 2, share=False)
+        project_out(STEPS - 1, share=False)

from contextlib import ExitStack

import concourse.mybir as mybir
from concourse.masks import make_identity

F32 = mybir.dt.float32
BF16 = mybir.dt.bfloat16
U8 = mybir.dt.uint8
U32 = mybir.dt.uint32
I32 = mybir.dt.int32
FP8 = mybir.dt.float8_e4m3fn
FP8X4 = mybir.dt.float8_e4m3fn_x4
FP4X4 = mybir.dt.float4_e2m1fn_x4
ADD = mybir.AluOpType.add
SUBTRACT = mybir.AluOpType.subtract
MULT = mybir.AluOpType.mult
MAX = mybir.AluOpType.max
ACT = mybir.ActivationFunctionType
X_AXIS = mybir.AxisListType.X

IMAGES, RES, C = 4, 32, 512
P = 128
NT = 4
SLOTS = RES * RES // P
QUARTERS = RES // SLOTS
STEP_SLOTS = 2
STEP_COLS = STEP_SLOTS * P
STEPS = IMAGES * SLOTS // STEP_SLOTS
GROUPS = STEPS // 2
GROUP_SLOTS = 2 * STEP_SLOTS
F_LAG = 3
FLOPS = 2 * 4 * IMAGES * RES * RES * C * C

WH, WW, WC, WP = 0, 1, 2, 3
BRANCH = {"x": ("L", 0, WC), "w": ("E", 0, WW), "h": ("E", 1, WH)}


def tile_dynamixerblock_pb_w4_kernel(
    tc,
    y_h,
    y_w_bytes,
    y_w_scale,
    x,
    a_logits,
    wo_h_words,
    wo_h_scales,
    bo_h,
    wo_w_words,
    wo_w_scales,
    bo_w,
    wmlpc_words,
    wmlpc_scales,
    wp_words,
    wp_scales,
    bp,
    out,
):
    nc = tc.nc
    x_rows = x.rearrange("b i j c -> b (i j) c")
    yw_rows = y_w_bytes.rearrange("(b i) j c -> b (i j) c", b=IMAGES)
    out_rows = out.rearrange("b i j c -> b (i j) c")

    with ExitStack() as ctx:
        const = ctx.enter_context(tc.tile_pool(name="const", bufs=1))
        stream = ctx.enter_context(tc.tile_pool(name="stream", bufs=3))
        psum = ctx.enter_context(tc.psum_pool(name="psum", bufs=8))
        ctx.enter_context(tc.manual_schedule())

        ident = const.tile([P, P], F32, name="ident")
        regroup = const.tile([P, P], F32, name="regroup")
        warm = const.tile([P, 1], F32, name="warm")
        w_raw = const.tile([P, 4, 2 * C], U8, name="w_raw", align_bytes=64)
        s_raw = const.tile([P, 4, C], U8, name="s_raw", align_bytes=64)
        w_perm = const.tile([P, 3, 2 * C], U8, name="w_perm", align_bytes=64)
        s_perm = const.tile([P, 3, C], U8, name="s_perm", align_bytes=64)
        logits = const.tile([P, IMAGES, NT, 3], BF16, name="logits")
        top = const.tile([P, IMAGES, NT], F32, name="top")
        total = const.tile([P, IMAGES, NT], F32, name="total")
        coef = const.tile([P, IMAGES, NT, 3], F32, name="coef")
        beta = const.tile([P, IMAGES, NT], F32, name="beta")
        beta_w = const.tile([P, IMAGES, NT], F32, name="beta_w")
        bias_h = const.tile([P, NT], BF16, name="bias_h")
        bias_w = const.tile([P, NT], BF16, name="bias_w")
        bias_p = const.tile([P, C], BF16, name="bias_p")
        yw_scale = const.tile([P, STEP_SLOTS, C], F32, name="yw_scale")
        x_sb, yh_sb, yw_sb = [], [], []
        for b in range(IMAGES):
            x_b = const.tile([P, SLOTS, C], BF16, name="x_sb%d" % b)
            yh_b = const.tile([P, SLOTS, C], BF16, name="yh_sb%d" % b)
            yw_b = const.tile([P, SLOTS, C], U8, name="yw_sb%d" % b)
            x_sb.append(x_b)
            yh_sb.append(yh_b)
            yw_sb.append(yw_b)

        def load_x(b, s0, s1):
            nc.sync.dma_start(
                out=x_sb[b][:, s0:s1, :], in_=x_rows[b].rearrange("(p s) c -> p s c", s=SLOTS)[:, s0:s1, :]
            )

        def load_yw(b, s0, s1):
            nc.sync.dma_start(
                out=yw_sb[b][:, s0:s1, :], in_=yw_rows[b].rearrange("(p s) c -> p s c", s=SLOTS)[:, s0:s1, :]
            )

        def load_yh(b, s0, s1, queue):
            for q in range(QUARTERS):
                first = b * RES + SLOTS * q
                queue.dma_start(
                    out=yh_sb[b][RES * q : RES * (q + 1), s0:s1, :],
                    in_=y_h[first + s0 : first + s1].rearrange("s i c -> i s c"),
                )

        def load_image(b):
            load_x(b, 0, SLOTS)
            load_yw(b, 0, SLOTS)
            load_yh(b, 0, SLOTS, nc.sync)

        def load_words(n, words):
            nc.sync.dma_start(out=w_raw[:, n, :], in_=words[0])

        def load_scales(n, scales):
            for q in range(4):
                nc.sync.dma_start(
                    out=s_raw[32 * q : 32 * q + 4, n, :].bitcast(I32), in_=scales[0, 4 * q : 4 * q + 4, :].bitcast(I32)
                )

        def permute_words(n):
            nc.vector.tensor_copy(
                out=w_perm[:, n, :].rearrange("p (t m e) -> p t m e", t=NT, e=2),
                in_=w_raw[:, n, :].rearrange("p (m t e) -> p t m e", t=NT, e=2),
            )

        def permute_scales(n):
            nc.vector.tensor_copy(
                out=s_perm[:, n, :].rearrange("p (t m) -> p t m", t=NT),
                in_=s_raw[:, n, :].rearrange("p (m t) -> p t m", t=NT),
            )

        wide, turned, pairs, codes_of = {}, {}, {}, {}

        def place(k):
            return divmod(k * STEP_SLOTS, SLOTS)

        def widen_yw(k):
            b, s0 = place(k)
            yw = stream.tile([P, STEP_SLOTS, C], BF16, name="yw_wide")
            nc.vector.tensor_tensor(
                out=yw[:].rearrange("p s c -> p (s c)"),
                in0=yw_sb[b][:, s0 : s0 + STEP_SLOTS, :].rearrange("p s c -> p (s c)").bitcast(FP8),
                in1=yw_scale[:].rearrange("p s c -> p (s c)"),
                op=MULT,
            )
            wide[k] = yw

        def turn(k, branch):
            b, s0 = place(k)
            src = {"x": x_sb[b], "h": yh_sb[b]}[branch][:, s0 : s0 + STEP_SLOTS, :] if branch != "w" else wide.pop(k)[:]
            bank = psum.tile([P, 2, STEP_SLOTS, P], F32, name="bank", tag="bank")
            for s in range(STEP_SLOTS):
                words = src[:, s, :].bitcast(F32)
                for u in range(2):
                    nc.tensor.transpose(
                        bank[:, u, s, :], words[:, u : C // 2 : 2], regroup[:] if branch == "h" else ident[:]
                    )
            turned[k, branch] = bank

        def pair(name, g):
            if (name, g) not in pairs:
                operands = stream.tile([P, 2, C, NT], BF16, name="pair_" + name, align_bytes=64)
                pairs[name, g] = operands
            return pairs[name, g]

        def group_cols(k):
            return slice(STEP_COLS * (k % 2), STEP_COLS * (k % 2 + 1))

        def collect(k, branch):
            name, i, n = BRANCH[branch]
            dst = pair(name, k // 2)[:, i, group_cols(k), :].rearrange("p n t -> p (n t)").bitcast(F32)
            nc.scalar.copy(
                out=dst.rearrange("p (n u) -> p n u", u=2), in_=turned.pop((k, branch))[:].rearrange("p u s r -> p (s r) u")
            )

        def bring(k, branch):
            turn(k, branch)
            collect(k, branch)

        def quantize(name, g, i0, i1, cols=slice(0, C)):
            if (name, g) not in codes_of:
                codes = stream.tile([P, 2, C], U32, name="codes_" + name, align_bytes=64)
                scales = stream.tile([P, 2, C], U8, name="scales_" + name, align_bytes=64)
                codes_of[name, g] = (codes, scales)
            codes, scales = codes_of[name, g]
            nc.vector.quantize_mx(
                out=codes[:, i0:i1, cols].rearrange("p i c -> p (i c)").bitcast(FP8X4),
                scales=scales[:, i0:i1, cols].rearrange("p i c -> p (i c)"),
                in_=pair(name, g)[:, i0:i1, cols, :].rearrange("p i n t -> p (i n t)"),
            )

        def quantize_f(k):
            quantize("L", k // 2 + F_LAG, 1, 2, group_cols(k))

        partial, planes = {}, {}

        def project(g, t, branch, cols):
            name, i, n = BRANCH[branch]
            codes, scales = codes_of[name, g]
            acc = psum.tile([P, C], F32, name="acc", tag="bank")
            nc.tensor.matmul_mx(
                out=acc[:, 0 : cols.stop - cols.start],
                lhsT=w_perm[:, n, 2 * P * t : 2 * P * (t + 1)].bitcast(FP4X4),
                lhsT_scale=s_perm[:, n, P * t : P * (t + 1)],
                rhs=codes[:, i, cols].bitcast(FP8X4),
                rhs_scale=scales[:, i, cols],
                start=True,
                stop=True,
            )
            return acc

        def add_branch(g, t, branch, cols):
            b = g * GROUP_SLOTS // SLOTS
            width = cols.stop - cols.start
            acc = project(g, t, branch, cols)[:, 0:width]
            if branch == "x":
                c_part = stream.tile([P, C], F32, name="c_part", bufs=4)
                partial[t] = c_part
                nc.scalar.activation(
                    out=c_part[:, 0:width],
                    in_=acc,
                    func=ACT.Identity,
                    bias=beta[:, b, t : t + 1],
                    scale=coef[:, b, t, 2:3],
                )
                return
            if branch == "w":
                cw_part = stream.tile([P, C], F32, name="cw_part", bufs=4)
                dst, a = cw_part[:, 0:width], coef[:, b, t, 1:2]
            else:
                if g not in planes:
                    f_planes = stream.tile([P, NT, C], BF16, name="f_planes")
                    planes[g] = f_planes
                dst, a = planes[g][:, t, cols], coef[:, b, t, 0:1]
            nc.vector.scalar_tensor_tensor(
                out=dst, in0=acc, scalar=a, in1=partial[t][:, 0:width], op0=MULT, op1=ADD
            )
            if branch == "w":
                partial[t] = cw_part

        def add_branches(k, branches):
            for branch in branches:
                for t in (2 * (k % 2), 2 * (k % 2) + 1):
                    add_branch(k // 2, t, branch, slice(0, C))

        def interleave(k):
            cols = group_cols(k)
            nc.scalar.copy(
                out=pair("L", k // 2 + F_LAG)[:, 1, cols, :].rearrange("p (n r) t -> p n t r", r=4),
                in_=planes[k // 2][:, :, cols].rearrange("p t (n r) -> p n t r", r=4),
            )

        def project_out(k, share):
            b, s0 = place(k)
            codes, scales = codes_of["L", k // 2 + F_LAG]
            o = stream.tile([P, STEP_SLOTS, C], F32, name="o", bufs=4)
            dst = out_rows[b].rearrange("(p s) c -> p s c", s=SLOTS)
            for s in range(STEP_SLOTS):
                tokens = slice(STEP_COLS * (k % 2) + P * s, STEP_COLS * (k % 2) + P * (s + 1))
                acc = psum.tile([P, C], F32, name="acc", tag="bank")
                nc.tensor.matmul_mx(
                    out=acc[:],
                    lhsT=codes[:, 1, tokens].bitcast(FP8X4),
                    lhsT_scale=scales[:, 1, tokens],
                    rhs=w_raw[:, WP, :].bitcast(FP4X4),
                    rhs_scale=s_raw[:, WP, :],
                    start=True,
                    stop=True,
                )
                if share and s == 1:
                    plain = stream.tile([P, C], F32, name="plain")
                    nc.scalar.copy(out=plain[:], in_=acc[:])
                    nc.gpsimd.tensor_tensor(out=o[:, s, :], in0=plain[:], in1=bias_p[:], op=ADD)
                else:
                    nc.vector.tensor_tensor(out=o[:, s, :], in0=acc[:], in1=bias_p[:], op=ADD)
                if k == STEPS - 1:
                    nc.sync.dma_start(out=dst[:, s0 + s, :], in_=o[:, s, :])
            if k < STEPS - 1:
                nc.sync.dma_start(out=dst[:, s0 : s0 + STEP_SLOTS, :], in_=o[:])

        nc.vector.memset(s_raw[:].rearrange("p n c -> p (n c)").bitcast(I32), 0)
        nc.vector.memset(warm[:], 0.0)
        nc.scalar.dma_start(
            out=logits[:].rearrange("p b t k -> p b (t k)"), in_=a_logits.rearrange("b (p x) -> p b x", p=P)
        )
        nc.scalar.dma_start(out=yw_scale[:, 0, :], in_=y_w_scale.rearrange("a o c -> (a o c)").partition_broadcast(P))
        nc.scalar.dma_start(out=bias_h[:], in_=bo_h.rearrange("(p t) -> p t", p=P))
        nc.scalar.dma_start(out=bias_w[:], in_=bo_w.rearrange("(p t) -> p t", p=P))
        nc.scalar.activation(out=warm[:], in_=warm[:], func=ACT.Exp)
        make_identity(nc, ident[:])
        nc.vector.tensor_copy(
            out=regroup[:].rearrange("p (i q) -> p q i", q=QUARTERS), in_=ident[:].rearrange("p (q i) -> p q i", q=QUARTERS)
        )
        load_yh(0, 0, GROUP_SLOTS, nc.gpsimd)
        load_yh(0, GROUP_SLOTS, SLOTS, nc.gpsimd)
        nc.gpsimd.dma_start(out=bias_p[:], in_=bp.partition_broadcast(P))
        load_scales(WC, wmlpc_scales)
        load_x(0, 0, 2)
        load_yw(0, 0, 4)
        load_words(WC, wmlpc_words)
        load_x(0, 2, 4)
        load_scales(WW, wo_w_scales)
        load_scales(WH, wo_h_scales)
        load_words(WW, wo_w_words)
        load_words(WH, wo_h_words)
        load_yw(0, 4, 8)
        load_x(0, 4, 8)
        load_image(1)
        load_scales(WP, wp_scales)
        load_words(WP, wp_words)
        flat = "p b t k -> p (b t) k"
        top_b = top[:].rearrange("p b t -> p (b t)").unsqueeze(2).to_broadcast([P, IMAGES * NT, 3])
        total_b = total[:].rearrange("p b t -> p (b t)").unsqueeze(2).to_broadcast([P, IMAGES * NT, 3])
        nc.vector.tensor_reduce(
            out=top[:].rearrange("p b t -> p (b t)"), in_=logits[:].rearrange(flat), axis=X_AXIS, op=MAX
        )
        nc.vector.tensor_tensor(out=coef[:].rearrange(flat), in0=logits[:].rearrange(flat), in1=top_b, op=SUBTRACT)
        nc.scalar.activation(
            out=coef[:].rearrange("p b t k -> p (b t k)"), in_=coef[:].rearrange("p b t k -> p (b t k)"), func=ACT.Exp
        )
        nc.vector.tensor_reduce(
            out=total[:].rearrange("p b t -> p (b t)"), in_=coef[:].rearrange(flat), axis=X_AXIS, op=ADD
        )
        nc.vector.reciprocal(out=total[:], in_=total[:])
        nc.vector.tensor_tensor(out=coef[:].rearrange(flat), in0=coef[:].rearrange(flat), in1=total_b, op=MULT)
        nc.vector.tensor_tensor(
            out=beta[:], in0=coef[:, :, :, 0], in1=bias_h[:].unsqueeze(1).to_broadcast([P, IMAGES, NT]), op=MULT
        )
        nc.vector.tensor_tensor(
            out=beta_w[:], in0=coef[:, :, :, 1], in1=bias_w[:].unsqueeze(1).to_broadcast([P, IMAGES, NT]), op=MULT
        )
        nc.vector.tensor_tensor(out=beta[:], in0=beta[:], in1=beta_w[:], op=ADD)
        nc.scalar.copy(out=yw_scale[:, 1, :], in_=yw_scale[:, 0, :])

        bring(0, "x")
        widen_yw(0)
        permute_words(WC)
        permute_scales(WC)
        bring(0, "w")
        bring(1, "x")
        widen_yw(1)
        bring(0, "h")
        bring(1, "w")
        quantize("L", 0, 0, 1)
        bring(1, "h")
        permute_words(WW)
        permute_scales(WW)
        quantize("E", 0, 0, 1)
        add_branches(0, "x")
        bring(2, "x")
        permute_words(WH)
        permute_scales(WH)
        quantize("E", 0, 1, 2)
        widen_yw(2)
        add_branches(0, "w")
        bring(2, "h")
        add_branches(0, "h")
        add_branches(1, "x")
        turn(2, "w")
        turn(3, "x")
        collect(2, "w")
        collect(3, "x")
        widen_yw(3)
        add_branches(1, "w")
        bring(3, "h")
        add_branches(1, "h")
        bring(3, "w")
        load_image(2)
        widen_yw(4)
        quantize("L", 1, 0, 1)
        quantize("E", 1, 0, 2)
        for branch in "xhw":
            turn(4, branch)
        for branch in "xhw":
            collect(4, branch)
        widen_yw(5)
        for k in range(2, STEPS - 2):
            g, odd = k // 2, k % 2
            if k == 5:
                load_image(3)
            if odd and g + 1 < GROUPS:
                quantize("L", g + 1, 0, 2 if g + 1 >= F_LAG else 1)
                quantize("E", g + 1, 0, 2)
            if k == 2:
                add_branches(k, "x")
            if k + 4 < STEPS:
                widen_yw(k + 4)
            if k + 3 < STEPS:
                for branch in "xhw":
                    turn(k + 3, branch)
                for branch in "xhw":
                    collect(k + 3, branch)
            if k > 2:
                add_branches(k, "x")
            if k >= 5:
                project_out(k - 5, share=True)
            add_branches(k, "wh")
            interleave(k - 2)

        for k in (STEPS - 2, STEPS - 1):
            def half(branch, *tiles):
                for t in tiles:
                    add_branch(GROUPS - 1, t, branch, group_cols(k))

            quantize_f(k - 4)
            if k == STEPS - 1:
                quantize_f(k - 3)
            half("x", 0, 1)
            if k == STEPS - 2:
                project_out(k - 5, share=True)
            project_out(k - 4, share=True)
            if k == STEPS - 1:
                project_out(k - 3, share=True)
            half("w", 0, 1)
            half("x", 2, 3)
            half("h", 0, 1)
            half("w", 2, 3)
            half("h", 2, 3)
            interleave(k - 2)

        interleave(STEPS - 2)
        quantize_f(STEPS - 3)
        interleave(STEPS - 1)
        project_out(STEPS - 3, share=False)
        quantize_f(STEPS - 2)
        quantize_f(STEPS - 1)
        project_out(STEPS - 2, share=False)
        project_out(STEPS - 1, share=False)
